import numpy as np
import ml_dtypes


BF16 = ml_dtypes.bfloat16


def bf(x):
    return np.asarray(x, np.float32).astype(BF16)


def f64(x):
    return np.asarray(x).astype(np.float64)


E2M1 = np.array([0.0, 0.5, 1.0, 1.5, 2.0, 3.0, 4.0, 6.0, -0.0, -0.5, -1.0, -1.5, -2.0, -3.0, -4.0, -6.0])


def pack_weight(w, fmt):
    k, n = w.shape
    w = f64(bf(w)).reshape(k // 32, 32, n)
    amax = np.abs(w).max(1)
    if fmt == "e4m3":
        byte = np.frexp(amax)[1] - 1 + 127 - 7
    else:
        mant, ex = np.frexp(amax / 6.0)
        byte = np.where(mant > 0.5, ex, ex - 1) + 127
    byte = np.clip(np.where(amax > 0, byte, 1), 1, 254)
    scaled = (w * np.exp2(127.0 - byte)[:, None, :]).reshape(k, n).astype(np.float32)
    by_word = np.ascontiguousarray(scaled.reshape(k // 512, 128, 4, n).transpose(0, 1, 3, 2))
    if fmt == "e4m3":
        words = by_word.astype(ml_dtypes.float8_e4m3fn).view(np.uint8)
    else:
        c = by_word.astype(ml_dtypes.float4_e2m1fn).view(np.uint8) & 0xF
        words = c[..., 0::2] | (c[..., 1::2] << 4)
    return np.ascontiguousarray(words), np.ascontiguousarray(byte.astype(np.uint8).reshape(k // 512, 16, n))


def unpack_weight(words, scales, fmt):
    g, p, n, _ = words.shape
    if fmt == "e4m3":
        vals = np.ascontiguousarray(words).view(ml_dtypes.float8_e4m3fn).astype(np.float64)
    else:
        nib = np.empty((g, p, n, 4), np.uint8)
        nib[..., 0::2] = words & 0xF
        nib[..., 1::2] = words >> 4
        vals = E2M1[nib]
    vals = vals * np.repeat(np.exp2(scales.astype(np.float64) - 127.0), 8, axis=1)[..., None]
    return vals.transpose(0, 1, 3, 2).reshape(g * 512, n)

def pack4(w):
    words, scales = pack_weight(w, "e2m1")
    return words.reshape(words.shape[0], 128, -1), scales


def unpack4(words, scales):
    return unpack_weight(words.reshape(words.shape[0], 128, -1, 2), scales, "e2m1")


def kspread(k):
    return np.exp2(np.repeat(np.random.randint(-6, 7, k // 32), 32).astype(np.float64))


B, IN, H = 512, 2048, 1024


def sigmoid(v):
    return 1.0 / (1.0 + np.exp(-v))


def setup_inputs():
    s, t = kspread(IN), kspread(H)
    a = np.sqrt(2.0 / (IN + H))
    x = np.random.standard_normal((B, IN)) * s
    x_words, x_scales = pack4(x.T)
    h_prev = np.random.standard_normal((B, H)) * t
    h_prev_words, h_prev_scales = pack4(h_prev.T)
    m_prev = bf(np.random.standard_normal((B, H)) * 0.5)
    Wi_x_words, Wi_x_scales = pack4((np.random.standard_normal((H, IN)) * a / s).T)
    b_i = bf(np.random.standard_normal(H) * 0.3)
    Wi_h_words, Wi_h_scales = pack4((np.random.standard_normal((H, H)) * a / t).T)
    Wf_x_words, Wf_x_scales = pack4((np.random.standard_normal((H, IN)) * a / s).T)
    b_f = bf(2.0 + np.random.standard_normal(H) * 0.3)
    Wf_h_words, Wf_h_scales = pack4((np.random.standard_normal((H, H)) * a / t).T)
    return {
        "x_words": x_words,
        "x_scales": x_scales,
        "h_prev_words": h_prev_words,
        "h_prev_scales": h_prev_scales,
        "m_prev": m_prev,
        "Wi_x_words": Wi_x_words,
        "Wi_x_scales": Wi_x_scales,
        "b_i": b_i,
        "Wi_h_words": Wi_h_words,
        "Wi_h_scales": Wi_h_scales,
        "Wf_x_words": Wf_x_words,
        "Wf_x_scales": Wf_x_scales,
        "b_f": b_f,
        "Wf_h_words": Wf_h_words,
        "Wf_h_scales": Wf_h_scales,
    }


def reference(x_words, x_scales, h_prev_words, h_prev_scales, m_prev, Wi_x_words, Wi_x_scales, b_i, Wi_h_words, Wi_h_scales, Wf_x_words, Wf_x_scales, b_f, Wf_h_words, Wf_h_scales):
    xq = unpack4(x_words, x_scales).T
    hq = unpack4(h_prev_words, h_prev_scales).T
    i_tilde = (xq @ unpack4(Wi_x_words, Wi_x_scales)) + f64(b_i) + (hq @ unpack4(Wi_h_words, Wi_h_scales))
    f_aff = (xq @ unpack4(Wf_x_words, Wf_x_scales)) + f64(b_f) + (hq @ unpack4(Wf_h_words, Wf_h_scales))
    log_f = np.log(np.maximum(sigmoid(f_aff), 1e-8))
    m_t = np.maximum(log_f + f64(m_prev), i_tilde)
    i_prime = np.exp(i_tilde - m_t)
    f_prime = np.exp(log_f + f64(m_prev) - m_t)
    return m_t, i_prime, f_prime

from contextlib import ExitStack
import math

import concourse.mybir as mybir

F32 = mybir.dt.float32
BF16 = mybir.dt.bfloat16
U8 = mybir.dt.uint8
I32 = mybir.dt.int32
FP4 = mybir.dt.float4_e2m1fn_x4
ALU = mybir.AluOpType
ACT = mybir.ActivationFunctionType

B, IN, H = 512, 2048, 1024
FLOPS = 2 * B * (IN + H) * 2 * H

P = 128
UNIT = 512
X_PASSES = IN // 512
H_PASSES = H // 512
PASSES = X_PASSES + H_PASSES
BANKS = 8
SP_CAP = -math.log(1e-8)
Z_SAFE = -20.0

WARM_UP = 26

TENSOR_ORDER = "F0 F1 F2 F3 I0 I1 I2 I3 F4 F5 F6 F7 I4 I5 I6 I7".split(" ")

RELU_ON_SCALAR = (0, 2)

VECTOR_ORDER = ("z0 z1 z2 z3 "
                "it0 it1 w0 it2 d0 it3 ti0 w1 z4 d1 z5 ti1 tf1 "
                "z6 z7 m0 it4 m1 it5 w2 it6 d2 it7 ti2 w3 m2 d3 ti3 tf3 m3").split(" ")

STORE_ORDER = "i0 f0 i1 f1 m0 m1 i2 m2 f2 i3 m3 f3".split(" ")


def tile_slstmlayer_pa_kernel(
    tc, x_words, x_scales, h_prev_words, h_prev_scales, m_prev,
    Wi_x_words, Wi_x_scales, b_i, Wi_h_words, Wi_h_scales,
    Wf_x_words, Wf_x_scales, b_f, Wf_h_words, Wf_h_scales,
    out_0, out_1, out_2,
):
    nc = tc.nc
    with ExitStack() as ctx:
        sbuf = ctx.enter_context(tc.tile_pool(name="sbuf", bufs=1))
        psum = ctx.enter_context(tc.psum_pool(name="psum", bufs=1))
        ctx.enter_context(tc.manual_schedule())

        def codes_tile(name, passes):
            return sbuf.tile([P, passes, 2 * UNIT], U8, name=name, align_bytes=64)

        def plane_tile(name, passes, columns):
            return sbuf.tile([P, passes, columns], U8, name=name, align_bytes=64)

        x_first = codes_tile("x_first", 1)
        x_rest = codes_tile("x_rest", X_PASSES - 1)
        h_codes = codes_tile("h_codes", H_PASSES)
        act_codes = [x_first[:, 0, :]] + [x_rest[:, g, :] for g in range(X_PASSES - 1)] \
            + [h_codes[:, g, :] for g in range(H_PASSES)]
        x_planes = plane_tile("x_planes", X_PASSES, B)
        h_planes = plane_tile("h_planes", H_PASSES, B)
        act_planes = [x_planes[:, g, :] for g in range(X_PASSES)] + [h_planes[:, g, :] for g in range(H_PASSES)]

        w_words = {"f": (Wf_x_words, Wf_h_words), "i": (Wi_x_words, Wi_h_words)}
        w_scales = {"f": (Wf_x_scales, Wf_h_scales), "i": (Wi_x_scales, Wi_h_scales)}
        wf_first = codes_tile("wf_first", 1)
        wf_rest = codes_tile("wf_rest", X_PASSES - 1)
        wx_tile = {}
        wh_tile = {}
        w_codes = {}
        w_planes = {}
        wx_planes = {}
        wh_planes = {}
        for gate in ("f", "i"):
            wx_planes[gate] = plane_tile("wx_planes_" + gate, X_PASSES, H)
            wh_planes[gate] = plane_tile("wh_planes_" + gate, H_PASSES, H)
            w_planes[gate] = [wx_planes[gate][:, g, :] for g in range(X_PASSES)] \
                + [wh_planes[gate][:, g, :] for g in range(H_PASSES)]
            for c in (0, 1):
                wh_tile[gate, c] = codes_tile("wh_%s%d" % (gate, c), H_PASSES)
                if (gate, c) == ("f", 0):
                    over_x = [wf_first[:, 0, :]] + [wf_rest[:, g, :] for g in range(X_PASSES - 1)]
                else:
                    wx_tile[gate, c] = codes_tile("wx_%s%d" % (gate, c), X_PASSES)
                    over_x = [wx_tile[gate, c][:, g, :] for g in range(X_PASSES)]
                w_codes[gate, c] = over_x + [wh_tile[gate, c][:, g, :] for g in range(H_PASSES)]

        bias_rows = sbuf.tile([P, 2, H], BF16, name="bias_rows")
        row_of = {"f": 0, "i": 1}
        ones = sbuf.tile([P, P], BF16, name="ones")
        table_warm = sbuf.tile([P, 1], F32, name="table_warm")
        bias = {}
        for gate in ("f", "i"):
            for c in (0, 1):
                bias[gate, c] = sbuf.tile([P, UNIT], F32, name="bias_%s%d" % (gate, c))
        pf_floor = sbuf.tile([P, 2], F32, name="pf_floor")
        m_prev_sb = [sbuf.tile([P, 4, UNIT], BF16, name="m_prev_%d" % c) for c in (0, 1)]

        def pair_tiles(name):
            return [sbuf.tile([P, 2, UNIT], F32, name="%s_%d" % (name, p)) for p in range(4)]

        z_sb = pair_tiles("z")
        it_sb = pair_tiles("it")
        d_sb = pair_tiles("d")
        ti_sb = pair_tiles("ti")
        tf_sb = pair_tiles("tf")
        ip_sb = pair_tiles("ip")
        fp_sb = pair_tiles("fp")

        def flat(tile):
            return tile[:].rearrange("p a n -> p (a n)")

        queues = {"sync": [], "vector": [], "tensor": [], "scalar": []}
        reads = {}
        emit = {}

        def step(queue, key, needs, fn):
            queues[queue].append(key)
            reads[key] = list(needs)
            emit[key] = fn

        def load_codes(key, tile, words, first_pass, end_pass, c):
            step("sync", key, [], lambda: nc.sync.dma_start(
                out=tile[:].bitcast(I32),
                in_=words[first_pass:end_pass, :, 2 * UNIT * c:2 * UNIT * (c + 1)]
                .rearrange("g p n -> p g n").bitcast(I32)))

        def rows_of(key):
            return ["%s.%d" % (key, r) for r in range(4)]

        def load_planes(key, tile, scales):
            for r in range(4):
                step("sync", "%s.%d" % (key, r), ["zero_" + key], lambda r=r: nc.sync.dma_start(
                    out=tile[r:P:32, :, :].bitcast(I32),
                    in_=scales[:, r:16:4, :].rearrange("g q n -> q g n").bitcast(I32)))

        def load_m_prev(c):
            step("sync", "m_prev%d" % c, [], lambda: nc.sync.dma_start(
                out=m_prev_sb[c][:], in_=m_prev[:, UNIT * c:UNIT * (c + 1)].rearrange("(t p) n -> p t n", p=P)))

        load_codes("x_first", x_first, x_words, 0, 1, 0)
        load_codes("wf_first", wf_first, Wf_x_words, 0, 1, 0)
        load_planes("x_planes", x_planes, x_scales)
        load_planes("wx_planes_f", wx_planes["f"], Wf_x_scales)
        load_codes("x_rest", x_rest, x_words, 1, X_PASSES, 0)
        load_codes("wf_rest", wf_rest, Wf_x_words, 1, X_PASSES, 0)
        load_codes("h_codes", h_codes, h_prev_words, 0, H_PASSES, 0)
        load_codes("wh_f0", wh_tile["f", 0], Wf_h_words, 0, H_PASSES, 0)
        load_planes("h_planes", h_planes, h_prev_scales)
        load_planes("wh_planes_f", wh_planes["f"], Wf_h_scales)
        load_codes("wx_i0", wx_tile["i", 0], Wi_x_words, 0, X_PASSES, 0)
        load_codes("wh_i0", wh_tile["i", 0], Wi_h_words, 0, H_PASSES, 0)
        load_planes("wx_planes_i", wx_planes["i"], Wi_x_scales)
        load_planes("wh_planes_i", wh_planes["i"], Wi_h_scales)
        load_m_prev(0)
        for gate in ("f", "i"):
            load_codes("wx_%s1" % gate, wx_tile[gate, 1], w_words[gate][0], 0, X_PASSES, 1)
            load_codes("wh_%s1" % gate, wh_tile[gate, 1], w_words[gate][1], 0, H_PASSES, 1)
        load_m_prev(1)

        def loads_for(gate, c, g):
            if g >= X_PASSES:
                return ["h_codes", "wh_%s%d" % (gate, c)] + rows_of("h_planes") + rows_of("wh_planes_" + gate)
            planes = rows_of("x_planes") + rows_of("wx_planes_" + gate)
            if (gate, c) != ("f", 0):
                return ["x_first", "x_rest", "wx_%s%d" % (gate, c)] + planes
            return (["x_first", "wf_first"] if g == 0 else ["x_rest", "wf_rest"]) + planes

        def zero_planes(key, tile):
            step("vector", "zero_" + key, [], lambda: nc.vector.memset(tile[:].bitcast(I32), 0))

        step("vector", "ones", [], lambda: nc.vector.memset(ones[:], 1.0))
        step("vector", "zero_bias_rows", [], lambda: nc.vector.memset(bias_rows[:].bitcast(I32), 0))
        step("vector", "zero_table_warm", [], lambda: nc.vector.memset(table_warm[:], 0.0))
        zero_planes("x_planes", x_planes)
        zero_planes("wx_planes_f", wx_planes["f"])
        zero_planes("h_planes", h_planes)
        zero_planes("wh_planes_f", wh_planes["f"])
        zero_planes("wx_planes_i", wx_planes["i"])
        zero_planes("wh_planes_i", wh_planes["i"])

        for gate, vec in (("f", b_f), ("i", b_i)):
            step("scalar", "bias_row_" + gate, ["zero_bias_rows"], lambda gate=gate, vec=vec: nc.scalar.dma_start(
                out=bias_rows[0:1, row_of[gate], :], in_=vec.rearrange("(o n) -> o n", o=1)))
        step("scalar", "table_warm", ["zero_table_warm"], lambda: nc.scalar.activation(
            out=table_warm[:], in_=table_warm[:], func=ACT.Exp))

        acc = {}
        emptied_by = {}
        taken = [0]

        def next_bank(emptier):
            bank = taken[0] % BANKS
            taken[0] += 1
            before = [emptied_by[bank]] if bank in emptied_by else []
            emptied_by[bank] = emptier
            return bank, before

        def open_bank(key, bank):
            acc[key] = psum.tile([P, UNIT], F32, name="bank%d" % bank, tag="bank%d" % bank)

        def mx_pass(key, g):
            gate, u = key[0].replace("F", "f").replace("I", "i"), int(key[1])
            c, t = u // 4, u % 4
            nc.tensor.matmul_mx(
                out=acc[key][:],
                lhsT=act_codes[g][:, 2 * P * t:2 * P * (t + 1)].bitcast(FP4),
                lhsT_scale=act_planes[g][:, P * t:P * (t + 1)],
                rhs=w_codes[gate, c][g].bitcast(FP4),
                rhs_scale=w_planes[gate][g][:, UNIT * c:UNIT * (c + 1)],
                start=(g == 0), stop=(g == PASSES - 1))

        def group_loads(key, passes):
            gate, c = key[0].replace("F", "f").replace("I", "i"), int(key[1]) // 4
            return [load for g in passes for load in loads_for(gate, c, g)]

        def emptier_of(key):
            return ("z" if key[0] == "F" else "it") + key[1]

        def warm_up():
            open_bank("warm_up", warm_bank)
            for k in range(WARM_UP):
                nc.tensor.matmul(out=acc["warm_up"][:, 0:P], lhsT=ones[:], rhs=ones[:], start=True, stop=True)

        head_groups = TENSOR_ORDER[:4]
        head_bank = {}
        for key in head_groups:
            head_bank[key] = next_bank(emptier_of(key))[0]
        warm_bank = taken[0] % BANKS
        step("tensor", "warm_up", ["ones"], warm_up)

        for gate, c in (("f", 0), ("i", 0), ("f", 1), ("i", 1)):
            key = "bias_%s%d" % (gate, c)
            bank = next_bank("copy_" + key)[0]

            def spread(key=key, bank=bank, gate=gate, c=c):
                open_bank(key, bank)
                nc.tensor.matmul(out=acc[key][:], lhsT=ones[:],
                                 rhs=bias_rows[:, row_of[gate], UNIT * c:UNIT * (c + 1)], start=True, stop=True)
            step("tensor", key, ["warm_up", "bias_row_" + gate], spread)
            step("scalar", "copy_" + key, [key], lambda key=key, gate=gate, c=c: nc.scalar.copy(
                out=bias[gate, c][:], in_=acc[key][:]))

        for c in (0, 1):
            step("vector", "b_f_max%d" % c, ["copy_bias_f%d" % c], lambda c=c: nc.vector.tensor_reduce(
                out=pf_floor[:, c:c + 1], in_=bias["f", c][:], axis=mybir.AxisListType.X, op=ALU.max))
            step("vector", "pf_floor%d" % c, ["b_f_max%d" % c], lambda c=c: nc.vector.tensor_scalar(
                out=pf_floor[:, c:c + 1], in0=pf_floor[:, c:c + 1], scalar1=-1.0, scalar2=Z_SAFE,
                op0=ALU.mult, op1=ALU.add))

        def head_pass(key, g):
            def run():
                if g == 0:
                    open_bank(key, head_bank[key])
                mx_pass(key, g)
            step("tensor", key if g == PASSES - 1 else "%s.%d" % (key, g), group_loads(key, [g]), run)

        for g in range(X_PASSES):
            for key in head_groups:
                head_pass(key, g)
        for key in head_groups:
            for g in range(X_PASSES, PASSES):
                head_pass(key, g)

        for key in TENSOR_ORDER[4:]:
            bank, before = next_bank(emptier_of(key))

            def group(key=key, bank=bank):
                open_bank(key, bank)
                for g in range(PASSES):
                    mx_pass(key, g)
            step("tensor", key, before + group_loads(key, range(PASSES)), group)

        vector_steps = {}

        def unit_steps(u):
            p, j, c = u // 2, u % 2, u // 4
            vector_steps["z%d" % u] = (["F%d" % u, "pf_floor%d" % c], lambda: nc.vector.scalar_tensor_tensor(
                out=z_sb[p][:, j, :], in0=acc["F%d" % u][:], scalar=pf_floor[:, c:c + 1], in1=bias["f", c][:],
                op0=ALU.max, op1=ALU.add))
            vector_steps["it%d" % u] = (["I%d" % u, "copy_bias_i%d" % c], lambda: nc.vector.tensor_tensor(
                out=it_sb[p][:, j, :], in0=acc["I%d" % u][:], in1=bias["i", c][:], op=ALU.add))

        def pair_steps(p):
            c, t = p // 2, 2 * (p % 2)
            vector_steps["w%d" % p] = (["it%d" % (2 * p), "it%d" % (2 * p + 1), "m_prev%d" % c],
                                       lambda: nc.vector.tensor_tensor(
                out=flat(d_sb[p]), in0=flat(it_sb[p]),
                in1=m_prev_sb[c][:, t:t + 2, :].rearrange("p a n -> p (a n)"), op=ALU.subtract))
            vector_steps["d%d" % p] = (["sp%d" % p, "w%d" % p], lambda: nc.vector.scalar_tensor_tensor(
                out=flat(d_sb[p]), in0=flat(z_sb[p]), scalar=SP_CAP, in1=flat(d_sb[p]), op0=ALU.min, op1=ALU.add))
            vector_steps["ti%d" % p] = (["d%d" % p], lambda: nc.vector.tensor_scalar(
                out=flat(ti_sb[p]), in0=flat(d_sb[p]), scalar1=0.0, scalar2=None, op0=ALU.min))
            if p not in RELU_ON_SCALAR:
                vector_steps["tf%d" % p] = (["d%d" % p], lambda: nc.vector.tensor_scalar(
                    out=flat(tf_sb[p]), in0=flat(d_sb[p]), scalar1=-1.0, scalar2=0.0, op0=ALU.mult, op1=ALU.min))
            vector_steps["m%d" % p] = (["ti%d" % p], lambda: nc.vector.tensor_tensor(
                out=flat(it_sb[p]), in0=flat(it_sb[p]), in1=flat(ti_sb[p]), op=ALU.subtract))

        for u in range(8):
            unit_steps(u)
        for p in range(4):
            pair_steps(p)
        for key in VECTOR_ORDER:
            step("vector", key, vector_steps[key][0], vector_steps[key][1])

        def exp_minus_z(u):
            view = z_sb[u // 2][:, u % 2, :]
            step("scalar", "e%d" % u, ["z%d" % u], lambda: nc.scalar.activation(
                out=view, in_=view, func=ACT.Exp, scale=-1.0))

        def softplus(p):
            step("scalar", "sp%d" % p, ["e%d" % (2 * p), "e%d" % (2 * p + 1)], lambda: nc.scalar.activation(
                out=flat(z_sb[p]), in_=flat(z_sb[p]), func=ACT.Ln, bias=1.0))

        def outputs(p):
            step("scalar", "ip%d" % p, ["ti%d" % p], lambda: nc.scalar.activation(
                out=flat(ip_sb[p]), in_=flat(ti_sb[p]), func=ACT.Exp))
            if p in RELU_ON_SCALAR:
                step("scalar", "relu%d" % p, ["d%d" % p], lambda: nc.scalar.activation(
                    out=flat(tf_sb[p]), in_=flat(d_sb[p]), func=ACT.Relu))
                step("scalar", "fp%d" % p, ["relu%d" % p], lambda: nc.scalar.activation(
                    out=flat(fp_sb[p]), in_=flat(tf_sb[p]), func=ACT.Exp, scale=-1.0))
            else:
                step("scalar", "fp%d" % p, ["tf%d" % p], lambda: nc.scalar.activation(
                    out=flat(fp_sb[p]), in_=flat(tf_sb[p]), func=ACT.Exp))

        for u in range(4):
            exp_minus_z(u)
        softplus(0)
        softplus(1)
        for p in (0, 1):
            outputs(p)
            exp_minus_z(4 + 2 * p)
            exp_minus_z(5 + 2 * p)
        softplus(2)
        softplus(3)
        outputs(2)
        outputs(3)

        stored = {"m": (out_0, it_sb, "m"), "i": (out_1, ip_sb, "ip"), "f": (out_2, fp_sb, "fp")}
        for key in STORE_ORDER:
            out, tiles, made_by = stored[key[0]]
            p = int(key[1])
            c, t = p // 2, 2 * (p % 2)
            step("sync", "store_" + key, [made_by + key[1]], lambda out=out, tiles=tiles, p=p, c=c, t=t: nc.sync.dma_start(
                out=out[P * t:P * (t + 2), UNIT * c:UNIT * (c + 1)].rearrange("(j q) n -> q j n", q=P),
                in_=tiles[p][:]))

        written = set()
        at = {name: 0 for name in queues}
        left = sum(len(queue) for queue in queues.values())
        while left:
            progress = 0
            for name in ("sync", "vector", "tensor", "scalar"):
                queue = queues[name]
                if at[name] < len(queue) and all(key in written for key in reads[queue[at[name]]]):
                    key = queue[at[name]]
                    emit[key]()
                    written.add(key)
                    at[name] += 1
                    progress += 1
            assert progress, "the queues' orders contradict what the steps read"
            left -= progress
